import numpy as np
import ml_dtypes


def mxq(x, axis, fmt="e4m3"):
    dtype, down = {"e4m3": (ml_dtypes.float8_e4m3fn, 7), "e5m2": (ml_dtypes.float8_e5m2, 14)}[fmt]
    v = np.moveaxis(np.asarray(x, np.float32).astype(ml_dtypes.bfloat16).astype(np.float64), axis, -1)
    blocks = v.reshape(v.shape[:-1] + (-1, 32))
    amax = np.abs(blocks).max(-1, keepdims=True)
    byte = np.maximum(np.where(amax > 0, np.frexp(amax)[1] - 1 + 127, 0) - down, 1)
    scale = np.exp2(byte - 127.0)
    codes = (blocks / scale).astype(np.float32).astype(dtype).astype(np.float64)
    return np.moveaxis((codes * scale).reshape(v.shape), -1, axis)


WIDE = False


def mx_kscale(k):
    if not WIDE:
        return np.ones(k)
    levels = np.array([18, -18])
    if k % 512:
        return np.exp2(np.random.permutation(np.resize(levels, k // 32))).repeat(32)
    a = np.empty((k // 512, 16))
    for p in range(k // 512):
        a[p, :8] = np.random.permutation(np.resize(levels, 8))
        for g in range(8):
            far = levels[np.abs(levels - a[p, g]) >= 10]
            a[p, g + 8] = far[np.random.randint(len(far))]
    return np.exp2(a.ravel()).repeat(32)


BF16 = ml_dtypes.bfloat16


def bf(x):
    return np.asarray(x, np.float32).astype(BF16)


def f64(x):
    return np.asarray(x).astype(np.float64)


NTR, NTE, D = 512, 512, 1536


def setup_inputs():
    s = mx_kscale(NTR + NTE)[:, None]
    st, sc = s[:NTR], s[NTR:]
    u = mx_kscale(D)
    c = 1.0 / np.max(u)
    xt0 = bf(np.random.standard_normal((NTR, D)))
    xc0 = bf(np.random.standard_normal((NTE, D)))
    m0 = bf(np.random.standard_normal((D, D)) / np.sqrt(D))
    sM = f64(xt0) @ f64(m0)
    g0 = bf(np.random.standard_normal((NTR, D)) * np.exp2(np.random.randint(-6, 1, (NTR, 1))) / st * u * c)
    s1 = st[:, 0]
    g1 = bf(np.random.standard_normal(NTR) * np.exp2(np.random.randint(-6, 1, NTR)) / (s1 * np.maximum(s1, 1.0)) * c)
    g2 = bf(np.random.standard_normal(NTE) * np.exp2(np.random.randint(-6, 1, NTE)) / sc[:, 0] ** 2 * c)
    return {"x_train": bf(f64(xt0) * st * u),
            "x_test": bf(f64(xc0) * sc * u),
            "M": bf(f64(m0) / u),
            "sM": np.asarray(sM, np.float32),
            "grad_0": g0, "grad_1": g1, "grad_2": g2}


def reference(x_train, x_test, M, sM, grad_0, grad_1, grad_2):
    xs, xc = f64(x_train), f64(x_test)
    g1 = f64(grad_1)[:, None]
    ds = f64(grad_0) + g1 * xs
    dc = f64(grad_2)[:, None] * xc
    dx = (mxq(ds, 1, "e5m2") @ mxq(f64(M), 1, "e4m3").T) + g1 * f64(sM)
    xj = np.concatenate([xs, xc], axis=0)
    dj = np.concatenate([ds, dc], axis=0)
    dm = mxq(xj, 0, "e4m3").T @ mxq(dj, 0, "e5m2")
    return dx, dm

@@ -1,0 +1,278 @@
+from contextlib import ExitStack
+
+import concourse.mybir as mybir
+from concourse.masks import make_identity
+
+NTR, NTE, D = 512, 512, 1536
+FLOPS = 2 * NTR * D * D + 2 * (NTR + NTE) * D * D
+
+F32 = mybir.dt.float32
+BF16 = mybir.dt.bfloat16
+U32 = mybir.dt.uint32
+U8 = mybir.dt.uint8
+E4M3 = mybir.dt.float8_e4m3fn_x4
+E5M2 = mybir.dt.float8_e5m2_x4
+MULT = mybir.AluOpType.mult
+ADD = mybir.AluOpType.add
+
+P = 128
+PACK = 4
+CH = P * PACK
+NCH = D // CH
+TILES = CH // P
+TB = 3
+FB = 2
+KB = 6
+WSLOT = {"mT0": "slot_w", "mT1": "slot_m0", "mT2": "slot_m1"}
+RSLOT = ("slot_xc", "slot_f0", "slot_f1", "slot_g0", "slot_xt", "slot_m2")
+
+
+def tile_rbfnet_pa_v_kernel(tc, x_train, x_test, M, sM, grad_0, grad_1, grad_2, out_0, out_1):
+    nc = tc.nc
+    with ExitStack() as ctx:
+        keep = ctx.enter_context(tc.tile_pool(name="keep", bufs=1))
+        stage = ctx.enter_context(tc.tile_pool(name="stage", bufs=1))
+        psum = ctx.enter_context(tc.psum_pool(name="psum", bufs=1))
+        ctx.enter_context(tc.manual_schedule())
+
+        def cols(c):
+            return slice(c * CH, (c + 1) * CH)
+
+        def by_token(t):
+            return t.rearrange("(p j) w -> p j w", j=PACK)
+
+        def operand(name):
+            codes = [keep.tile([P, CH], U32, name="%s_codes%d" % (name, c), align_bytes=64) for c in range(NCH)]
+            scales = [keep.tile([P, CH], U8, name="%s_scales%d" % (name, c), align_bytes=64) for c in range(NCH)]
+            return codes, scales
+
+        def quantise(op, c, grouped, fmt):
+            nc.vector.quantize_mx(out=op[0][c][:].bitcast(fmt), scales=op[1][c][:], in_=grouped[:])
+
+        def copy(engine, out, in_):
+            if engine == "V":
+                nc.vector.tensor_copy(out=out, in_=in_)
+            else:
+                nc.scalar.copy(out=out, in_=in_)
+
+        ident = keep.tile([P, P], F32, name="ident")
+        make_identity(nc, ident[:])
+        g1 = keep.tile([P, PACK], BF16, name="g1")
+        g2 = keep.tile([P, PACK], BF16, name="g2")
+        nc.scalar.dma_start(out=g2[:], in_=grad_2.rearrange("(p j) -> p j", j=PACK))
+        nc.scalar.dma_start(out=g1[:], in_=grad_1.rearrange("(p j) -> p j", j=PACK))
+
+        raw = {}
+        src = {"xt": x_train, "xc": x_test, "g0": grad_0}
+        for name in src:
+            raw[name] = keep.tile([P, PACK, D], BF16, name=name + "_raw", tag="slot_" + name, align_bytes=64)
+        m_raw = [keep.tile([P, PACK, D], BF16, name="m_raw%d" % n, tag="slot_m%d" % n, align_bytes=64) for n in range(NCH)]
+        sm = [keep.tile([P, 2, D], F32, name="sm%d" % h) for h in range(2)]
+        ds = [keep.tile([P, PACK, CH], BF16, name="ds%d" % c) for c in range(NCH)]
+        q = {name: operand(name) for name in ("xt", "xc", "ds", "dc", "dsT", "mT0", "mT1", "mT2")}
+        grouped = {}
+        rows = {}
+        wide = {}
+        row_slots = ["slot_a", "slot_b", "slot_g0", "slot_xc", "slot_xt", "slot_m0"]
+        count = {"t": 0, "mm": 0}
+
+        def load(name, c0, c1):
+            w = slice(c0 * CH, c1 * CH)
+            nc.sync.dma_start(out=raw[name][:, :, w], in_=by_token(src[name])[:, :, w])
+
+        def load_m(n):
+            nc.sync.dma_start(out=m_raw[n][:], in_=by_token(M[cols(n), :]))
+
+        def load_sm(h):
+            nc.sync.dma_start(out=sm[h][:], in_=by_token(sM)[:, 2 * h : 2 * h + 2, :])
+
+        def new_grouped(key, tag, bufs):
+            grouped[key] = stage.tile([P, CH * PACK], BF16, name="grouped", tag=tag, bufs=bufs, align_bytes=64)
+            return grouped[key]
+
+        def interleave(name, c, engine):
+            rows_in = ds[c][:] if name == "ds" else raw[name][:, :, cols(c)]
+            dst = new_grouped((name, c), "tok", KB)
+            copy(engine, dst[:].rearrange("p (c i t) -> p c t i", i=4, t=PACK), rows_in.rearrange("p t (c i) -> p c t i", i=4))
+
+        def quant_tok(name, c):
+            quantise(q[name], c, grouped[name, c], E4M3 if name in ("xt", "xc") else E5M2)
+
+        def make_ds(c):
+            for j in range(PACK):
+                nc.vector.scalar_tensor_tensor(out=ds[c][:, j, :], in0=raw["xt"][:, j, cols(c)], scalar=g1[:, j : j + 1],
+                                               in1=raw["g0"][:, j, cols(c)], op0=MULT, op1=ADD)
+
+        def make_dc(c):
+            dst = new_grouped(("dc", c), "tok", KB)
+            nc.vector.tensor_tensor(out=dst[:].rearrange("p (w j) -> p w j", j=PACK),
+                                    in0=grouped["xc", c][:].rearrange("p (w j) -> p w j", j=PACK),
+                                    in1=g2[:].unsqueeze(1).broadcast_to([P, CH, PACK]), op=MULT)
+
+        def turn(name, g, engines):
+            source = ds[g] if name == "dsT" else m_raw[int(name[2])]
+            base = 0 if name == "dsT" else g * CH // 2
+            if name == "dsT":
+                dst = new_grouped((name, g), "feat", FB)
+            else:
+                if name not in wide:
+                    wide[name] = keep.tile([P, NCH * CH * PACK], BF16, name=name + "_grouped", tag=WSLOT[name], align_bytes=64)
+                dst = wide[name][:, g * CH * PACK : (g + 1) * CH * PACK]
+                grouped[name, g] = dst
+            words = dst[:].bitcast(F32)
+            banks = []
+            for b in range(2):
+                bank = psum.tile([P, 2, 2, P], F32, name="tbank", tag="tbank", bufs=TB)
+                banks.append(bank)
+                for r in range(2):
+                    row = source[:, 2 * b + r, :].bitcast(F32)
+                    for u in range(2):
+                        nc.tensor.transpose(bank[:, r, u, :], row[:, base + u : base + CH // 2 : 2], ident[:])
+            for b in range(2):
+                copy(engines[b], words[:, b * CH : (b + 1) * CH].rearrange("k (r p u) -> k r p u", r=2, u=2),
+                     banks[b][:].rearrange("k r u p -> k r p u"))
+
+        def quant_feat(name, g):
+            quantise(q[name], g, grouped[name, g], E5M2 if name == "dsT" else E4M3)
+
+        def mx(acc, left, lc, lw, lfmt, right, rc, rfmt, start, stop):
+            nc.tensor.matmul_mx(out=acc[:], lhsT=left[0][lc][:, lw].bitcast(lfmt), lhsT_scale=left[1][lc][:, lw],
+                                rhs=right[0][rc][:].bitcast(rfmt), rhs_scale=right[1][rc][:], start=start, stop=stop)
+
+        def dm_place(m, n):
+            if n == 0:
+                key = ("first", m // TILES)
+                if key not in rows:
+                    rows[key] = keep.tile([P, TILES, CH], F32, name="first%d" % key[1], tag="slot_f%d" % key[1], align_bytes=64)
+                return rows[key][:, m % TILES, :]
+            key = ("rest", m // 2)
+            if key not in rows:
+                rows[key] = keep.tile([P, 2, 2 * CH], F32, name="rest%d" % key[1], tag=RSLOT[key[1]], align_bytes=64)
+            return rows[key][:, m % 2, cols(n - 1)]
+
+        def dm_tile(m, n, engine):
+            w = slice((m % TILES) * P, (m % TILES + 1) * P)
+            acc = psum.tile([P, CH], F32, name="acc", tag="acc", bufs=8 - TB)
+            mx(acc, q["xc"], m // TILES, w, E4M3, q["dc"], n, E5M2, True, False)
+            mx(acc, q["xt"], m // TILES, w, E4M3, q["ds"], n, E5M2, False, True)
+            copy(engine, dm_place(m, n), acc[:])
+
+        def store_first(c):
+            nc.sync.dma_start(out=out_1[cols(c), cols(0)].rearrange("(m p) w -> p m w", p=P), in_=rows["first", c][:])
+
+        def store_rest(h):
+            nc.sync.dma_start(out=out_1[2 * h * P : 2 * (h + 1) * P, CH:].rearrange("(m p) w -> p m w", p=P), in_=rows["rest", h][:])
+
+        def store_rest_row(m, c0, c1):
+            nc.sync.dma_start(out=out_1[m * P : (m + 1) * P, c0 * CH : c1 * CH], in_=rows["rest", m // 2][:, m % 2, (c0 - 1) * CH : (c1 - 1) * CH])
+
+        def dx_tile(j, n):
+            acc = psum.tile([P, CH], F32, name="acc", tag="acc", bufs=8 - TB)
+            for g in range(NCH):
+                mx(acc, q["dsT"], g, slice(j * P, (j + 1) * P), E5M2, q["mT%d" % n], g, E4M3, g == 0, g == NCH - 1)
+            part = sm[j // 2][:, j % 2, cols(n)].rearrange("p (a r) -> p a r", r=PACK)
+            nc.vector.scalar_tensor_tensor(out=part, in0=part, scalar=g1[:, j : j + 1],
+                                           in1=acc[:].rearrange("p (r a) -> p a r", r=PACK), op0=MULT, op1=ADD)
+
+        def store_dx(j, c0, c1):
+            w = slice(c0 * CH, c1 * CH)
+            nc.sync.dma_start(out=by_token(out_0)[:, j, w], in_=sm[j // 2][:, j % 2, w])
+
+
+        load("xc", 0, 1)
+        load("xt", 0, 1)
+        load("g0", 0, 1)
+        load_m(0)
+        load("xc", 1, 3)
+        load("xt", 1, 3)
+        load_m(1)
+        load("g0", 1, 3)
+        load_m(2)
+        interleave("xc", 0, "V")
+        interleave("xt", 0, "S")
+        make_dc(0)
+        quant_tok("xc", 0)
+        quant_tok("dc", 0)
+        make_ds(0)
+        quant_tok("xt", 0)
+        interleave("ds", 0, "V")
+        turn("dsT", 0, "SS")
+        for g in range(3):
+            turn("mT0", g, "SS")
+        quant_feat("dsT", 0)
+        quant_tok("ds", 0)
+        interleave("xc", 1, "V")
+        for m in range(4):
+            dm_tile(m, 0, "S")
+        store_first(0)
+        make_dc(1)
+        quant_tok("xc", 1)
+        interleave("xt", 1, "V")
+        quant_tok("dc", 1)
+        quant_tok("xt", 1)
+        interleave("xc", 2, "V")
+        interleave("xt", 2, "V")
+        quant_tok("xc", 2)
+        quant_tok("xt", 2)
+        for m in range(4, 8):
+            dm_tile(m, 0, "S")
+        store_first(1)
+        make_ds(1)
+        turn("mT1", 0, "SS")
+        dm_tile(8, 0, "S")
+        dm_tile(9, 0, "S")
+        turn("mT1", 1, "SS")
+        dm_tile(10, 0, "S")
+        dm_tile(11, 0, "S")
+        turn("mT1", 2, "SS")
+        store_first(2)
+        load_sm(0)
+        load_sm(1)
+        make_dc(2)
+        interleave("ds", 1, "V")
+        quant_tok("dc", 2)
+        quant_tok("ds", 1)
+        make_ds(2)
+        turn("mT2", 0, "SS")
+        dm_tile(0, 1, "S")
+        dm_tile(1, 1, "S")
+        turn("mT2", 1, "SS")
+        dm_tile(2, 1, "S")
+        dm_tile(3, 1, "S")
+        turn("mT2", 2, "SS")
+        quant_feat("mT0", 0)
+        interleave("ds", 2, "V")
+        quant_feat("mT0", 1)
+        quant_tok("ds", 2)
+        quant_feat("mT0", 2)
+        for g in range(3):
+            quant_feat("mT1", g)
+        for m in range(4):
+            dm_tile(m, 2, "S")
+            if m % 2:
+                store_rest(m // 2)
+        turn("dsT", 1, "SS")
+        quant_feat("mT2", 0)
+        quant_feat("mT2", 1)
+        quant_feat("dsT", 1)
+        for m in range(4, 8):
+            dm_tile(m, 1, "S")
+            dm_tile(m, 2, "V" if m % 2 else "S")
+            if m % 2:
+                store_rest(m // 2)
+            if m == 5:
+                turn("dsT", 2, "SS")
+                quant_feat("mT2", 2)
+                quant_feat("dsT", 2)
+        for j in range(4):
+            for n in range(3):
+                dx_tile(j, n)
+            store_dx(j, 0, 3)
+            dm_tile(8 + j, 1, "S")
+            if j == 3:
+                store_rest_row(8 + j, 1, 2)
+            dm_tile(8 + j, 2, "S")
+            if j == 3:
+                store_rest_row(8 + j, 2, 3)
+            else:
+                store_rest_row(8 + j, 1, 3)

@@ -24,7 +24,7 @@ TB = 3
 FB = 2
 KB = 6
 WSLOT = {"mT0": "slot_w", "mT1": "slot_m0", "mT2": "slot_m1"}
-RSLOT = ("slot_xc", "slot_f0", "slot_f1", "slot_g0", "slot_xt", "slot_m2")
+RSLOT = ("slot_f0", "slot_f1", "slot_f2", "slot_g01", "slot_w", "slot_m2")
 
 
 def tile_rbfnet_pa_v_kernel(tc, x_train, x_test, M, sM, grad_0, grad_1, grad_2, out_0, out_1):
@@ -65,7 +65,7 @@ def tile_rbfnet_pa_v_kernel(tc, x_train, x_test, M, sM, grad_0, grad_1, grad_2, 
         raw = {}
         src = {"xt": x_train, "xc": x_test, "g0": grad_0}
         for name in src:
-            raw[name] = keep.tile([P, PACK, D], BF16, name=name + "_raw", tag="slot_" + name, align_bytes=64)
+            raw[name] = {}
         m_raw = [keep.tile([P, PACK, D], BF16, name="m_raw%d" % n, tag="slot_m%d" % n, align_bytes=64) for n in range(NCH)]
         sm = [keep.tile([P, 2, D], F32, name="sm%d" % h) for h in range(2)]
         ds = [keep.tile([P, PACK, CH], BF16, name="ds%d" % c) for c in range(NCH)]
@@ -73,12 +73,16 @@ def tile_rbfnet_pa_v_kernel(tc, x_train, x_test, M, sM, grad_0, grad_1, grad_2, 
         grouped = {}
         rows = {}
         wide = {}
+        opened = {}
         row_slots = ["slot_a", "slot_b", "slot_g0", "slot_xc", "slot_xt", "slot_m0"]
         count = {"t": 0, "mm": 0}
 
         def load(name, c0, c1):
             w = slice(c0 * CH, c1 * CH)
-            nc.sync.dma_start(out=raw[name][:, :, w], in_=by_token(src[name])[:, :, w])
+            part = keep.tile([P, PACK, (c1 - c0) * CH], BF16, name="%s_raw%d" % (name, c0), tag="slot_%s%d" % (name, c0), align_bytes=64)
+            nc.sync.dma_start(out=part[:], in_=by_token(src[name])[:, :, w])
+            for c in range(c0, c1):
+                raw[name][c] = part[:, :, cols(c - c0)]
 
         def load_m(n):
             nc.sync.dma_start(out=m_raw[n][:], in_=by_token(M[cols(n), :]))
@@ -91,7 +95,7 @@ def tile_rbfnet_pa_v_kernel(tc, x_train, x_test, M, sM, grad_0, grad_1, grad_2, 
             return grouped[key]
 
         def interleave(name, c, engine):
-            rows_in = ds[c][:] if name == "ds" else raw[name][:, :, cols(c)]
+            rows_in = ds[c][:] if name == "ds" else raw[name][c]
             dst = new_grouped((name, c), "tok", KB)
             copy(engine, dst[:].rearrange("p (c i t) -> p c t i", i=4, t=PACK), rows_in.rearrange("p t (c i) -> p c t i", i=4))
 
@@ -100,8 +104,8 @@ def tile_rbfnet_pa_v_kernel(tc, x_train, x_test, M, sM, grad_0, grad_1, grad_2, 
 
         def make_ds(c):
             for j in range(PACK):
-                nc.vector.scalar_tensor_tensor(out=ds[c][:, j, :], in0=raw["xt"][:, j, cols(c)], scalar=g1[:, j : j + 1],
-                                               in1=raw["g0"][:, j, cols(c)], op0=MULT, op1=ADD)
+                nc.vector.scalar_tensor_tensor(out=ds[c][:, j, :], in0=raw["xt"][c][:, j, :], scalar=g1[:, j : j + 1],
+                                               in1=raw["g0"][c][:, j, :], op0=MULT, op1=ADD)
 
         def make_dc(c):
             dst = new_grouped(("dc", c), "tok", KB)
@@ -150,11 +154,17 @@ def tile_rbfnet_pa_v_kernel(tc, x_train, x_test, M, sM, grad_0, grad_1, grad_2, 
                 rows[key] = keep.tile([P, 2, 2 * CH], F32, name="rest%d" % key[1], tag=RSLOT[key[1]], align_bytes=64)
             return rows[key][:, m % 2, cols(n - 1)]
 
+        def dm_open(m, n):
+            w = slice((m % TILES) * P, (m % TILES + 1) * P)
+            opened[m, n] = psum.tile([P, CH], F32, name="acc", tag="acc", bufs=8 - TB)
+            mx(opened[m, n], q["xt"], m // TILES, w, E4M3, q["ds"], n, E5M2, True, False)
+
         def dm_tile(m, n, engine):
             w = slice((m % TILES) * P, (m % TILES + 1) * P)
-            acc = psum.tile([P, CH], F32, name="acc", tag="acc", bufs=8 - TB)
-            mx(acc, q["xc"], m // TILES, w, E4M3, q["dc"], n, E5M2, True, False)
-            mx(acc, q["xt"], m // TILES, w, E4M3, q["ds"], n, E5M2, False, True)
+            if (m, n) not in opened:
+                dm_open(m, n)
+            acc = opened[m, n]
+            mx(acc, q["xc"], m // TILES, w, E4M3, q["dc"], n, E5M2, False, True)
             copy(engine, dm_place(m, n), acc[:])
 
         def store_first(c):
@@ -179,37 +189,39 @@ def tile_rbfnet_pa_v_kernel(tc, x_train, x_test, M, sM, grad_0, grad_1, grad_2, 
             nc.sync.dma_start(out=by_token(out_0)[:, j, w], in_=sm[j // 2][:, j % 2, w])
 
 
-        load("xc", 0, 1)
         load("xt", 0, 1)
         load("g0", 0, 1)
+        load("xc", 0, 1)
         load_m(0)
-        load("xc", 1, 3)
-        load("xt", 1, 3)
+        load("xc", 1, 2)
+        load("xt", 1, 2)
+        load("xc", 2, 3)
+        load("xt", 2, 3)
         load_m(1)
         load("g0", 1, 3)
         load_m(2)
-        interleave("xc", 0, "V")
-        interleave("xt", 0, "S")
-        make_dc(0)
-        quant_tok("xc", 0)
-        quant_tok("dc", 0)
+        interleave("xt", 0, "V")
+        interleave("xc", 0, "S")
         make_ds(0)
         quant_tok("xt", 0)
         interleave("ds", 0, "V")
         turn("dsT", 0, "SS")
-        for g in range(3):
-            turn("mT0", g, "SS")
-        quant_feat("dsT", 0)
+        quant_tok("xc", 0)
         quant_tok("ds", 0)
+        make_dc(0)
         interleave("xc", 1, "V")
+        quant_tok("dc", 0)
+        turn("mT0", 0, "SS")
+        for m in range(4):
+            dm_open(m, 0)
+        turn("mT0", 1, "SS")
+        interleave("xt", 1, "V")
+        quant_tok("xc", 1)
+        quant_tok("xt", 1)
         for m in range(4):
             dm_tile(m, 0, "S")
+        turn("mT0", 2, "SS")
         store_first(0)
-        make_dc(1)
-        quant_tok("xc", 1)
-        interleave("xt", 1, "V")
-        quant_tok("dc", 1)
-        quant_tok("xt", 1)
         interleave("xc", 2, "V")
         interleave("xt", 2, "V")
         quant_tok("xc", 2)
@@ -217,22 +229,26 @@ def tile_rbfnet_pa_v_kernel(tc, x_train, x_test, M, sM, grad_0, grad_1, grad_2, 
         for m in range(4, 8):
             dm_tile(m, 0, "S")
         store_first(1)
+        make_dc(1)
+        quant_feat("dsT", 0)
+        quant_tok("dc", 1)
         make_ds(1)
-        turn("mT1", 0, "SS")
         dm_tile(8, 0, "S")
         dm_tile(9, 0, "S")
-        turn("mT1", 1, "SS")
+        turn("mT1", 0, "SS")
         dm_tile(10, 0, "S")
+        turn("mT1", 1, "SS")
         dm_tile(11, 0, "S")
         turn("mT1", 2, "SS")
         store_first(2)
         load_sm(0)
         load_sm(1)
-        make_dc(2)
+        quant_feat("mT0", 0)
         interleave("ds", 1, "V")
-        quant_tok("dc", 2)
+        quant_feat("mT0", 1)
         quant_tok("ds", 1)
         make_ds(2)
+        make_dc(2)
         turn("mT2", 0, "SS")
         dm_tile(0, 1, "S")
         dm_tile(1, 1, "S")
@@ -240,9 +256,9 @@ def tile_rbfnet_pa_v_kernel(tc, x_train, x_test, M, sM, grad_0, grad_1, grad_2, 
         dm_tile(2, 1, "S")
         dm_tile(3, 1, "S")
         turn("mT2", 2, "SS")
-        quant_feat("mT0", 0)
+        turn("dsT", 1, "SS")
         interleave("ds", 2, "V")
-        quant_feat("mT0", 1)
+        quant_tok("dc", 2)
         quant_tok("ds", 2)
         quant_feat("mT0", 2)
         for g in range(3):
@@ -251,7 +267,6 @@ def tile_rbfnet_pa_v_kernel(tc, x_train, x_test, M, sM, grad_0, grad_1, grad_2, 
             dm_tile(m, 2, "S")
             if m % 2:
                 store_rest(m // 2)
-        turn("dsT", 1, "SS")
         quant_feat("mT2", 0)
         quant_feat("mT2", 1)
         quant_feat("dsT", 1)

@@ -20,274 +20,216 @@ PACK = 4
 CH = P * PACK
 NCH = D // CH
 TILES = CH // P
-TB = 3
-FB = 2
-KB = 6
-WSLOT = {"mT0": "slot_w", "mT1": "slot_m0", "mT2": "slot_m1"}
-RSLOT = ("slot_f0", "slot_f1", "slot_f2", "slot_g01", "slot_w", "slot_m2")
+ALIGN = 64
+FORMAT = {"xt": E4M3, "xc": E4M3, "mT0": E4M3, "mT1": E4M3, "mT2": E4M3, "ds": E5M2, "dc": E5M2, "dsT": E5M2}
+
+BANKS = 8
+TOKEN_BUFS = 5
+DS_BUFS = 2
+BLOCK_BUFS = 5
+WEAVE = 2
+VECTOR_SHARE = 3
 
 
 def tile_rbfnet_pa_v_kernel(tc, x_train, x_test, M, sM, grad_0, grad_1, grad_2, out_0, out_1):
     nc = tc.nc
     with ExitStack() as ctx:
-        keep = ctx.enter_context(tc.tile_pool(name="keep", bufs=1))
-        stage = ctx.enter_context(tc.tile_pool(name="stage", bufs=1))
-        psum = ctx.enter_context(tc.psum_pool(name="psum", bufs=1))
+        sbuf = ctx.enter_context(tc.tile_pool(name="sbuf", bufs=1))
+        psum = ctx.enter_context(tc.psum_pool(name="psum", bufs=BANKS))
         ctx.enter_context(tc.manual_schedule())
 
         def cols(c):
             return slice(c * CH, (c + 1) * CH)
 
-        def by_token(t):
+        def four_rows(t):
             return t.rearrange("(p j) w -> p j w", j=PACK)
 
-        def operand(name):
-            codes = [keep.tile([P, CH], U32, name="%s_codes%d" % (name, c), align_bytes=64) for c in range(NCH)]
-            scales = [keep.tile([P, CH], U8, name="%s_scales%d" % (name, c), align_bytes=64) for c in range(NCH)]
-            return codes, scales
-
-        def quantise(op, c, grouped, fmt):
-            nc.vector.quantize_mx(out=op[0][c][:].bitcast(fmt), scales=op[1][c][:], in_=grouped[:])
-
         def copy(engine, out, in_):
-            if engine == "V":
+            if engine == "vector":
                 nc.vector.tensor_copy(out=out, in_=in_)
             else:
                 nc.scalar.copy(out=out, in_=in_)
 
-        ident = keep.tile([P, P], F32, name="ident")
+        ident = sbuf.tile([P, P], F32, name="ident")
         make_identity(nc, ident[:])
-        g1 = keep.tile([P, PACK], BF16, name="g1")
-        g2 = keep.tile([P, PACK], BF16, name="g2")
-        nc.scalar.dma_start(out=g2[:], in_=grad_2.rearrange("(p j) -> p j", j=PACK))
+        g1 = sbuf.tile([P, PACK], BF16, name="g1")
+        g2 = sbuf.tile([P, PACK], BF16, name="g2")
         nc.scalar.dma_start(out=g1[:], in_=grad_1.rearrange("(p j) -> p j", j=PACK))
+        nc.scalar.dma_start(out=g2[:], in_=grad_2.rearrange("(p j) -> p j", j=PACK))
 
-        raw = {}
-        src = {"xt": x_train, "xc": x_test, "g0": grad_0}
-        for name in src:
-            raw[name] = {}
-        m_raw = [keep.tile([P, PACK, D], BF16, name="m_raw%d" % n, tag="slot_m%d" % n, align_bytes=64) for n in range(NCH)]
-        sm = [keep.tile([P, 2, D], F32, name="sm%d" % h) for h in range(2)]
-        ds = [keep.tile([P, PACK, CH], BF16, name="ds%d" % c) for c in range(NCH)]
-        q = {name: operand(name) for name in ("xt", "xc", "ds", "dc", "dsT", "mT0", "mT1", "mT2")}
-        grouped = {}
-        rows = {}
-        wide = {}
-        opened = {}
-        row_slots = ["slot_a", "slot_b", "slot_g0", "slot_xc", "slot_xt", "slot_m0"]
-        count = {"t": 0, "mm": 0}
+        codes, scales = {}, {}
+        for name in FORMAT:
+            for c in range(NCH):
+                codes[name, c] = sbuf.tile([P, CH], U32, name="%s_codes%d" % (name, c), align_bytes=ALIGN)
+                scales[name, c] = sbuf.tile([P, CH], U8, name="%s_scales%d" % (name, c), align_bytes=ALIGN)
+        loaded, grouped, blocks, saved = {}, {}, {}, {}
 
-        def load(name, c0, c1):
-            w = slice(c0 * CH, c1 * CH)
-            part = keep.tile([P, PACK, (c1 - c0) * CH], BF16, name="%s_raw%d" % (name, c0), tag="slot_%s%d" % (name, c0), align_bytes=64)
-            nc.sync.dma_start(out=part[:], in_=by_token(src[name])[:, :, w])
-            for c in range(c0, c1):
-                raw[name][c] = part[:, :, cols(c - c0)]
+        def load_tokens(name, source, c):
+            loaded[name, c] = sbuf.tile([P, PACK, CH], BF16, name=name, tag="%s%d" % (name, c), align_bytes=ALIGN)
+            nc.sync.dma_start(out=loaded[name, c][:], in_=four_rows(source)[:, :, cols(c)])
 
-        def load_m(n):
-            nc.sync.dma_start(out=m_raw[n][:], in_=by_token(M[cols(n), :]))
+        def load_m(n, half):
+            loaded["m", n, half] = sbuf.tile([P, 2, D], BF16, name="m", tag="m%d_%d" % (n, half), align_bytes=ALIGN)
+            nc.sync.dma_start(out=loaded["m", n, half][:], in_=four_rows(M[cols(n), :])[:, 2 * half : 2 * half + 2, :])
 
-        def load_sm(h):
-            nc.sync.dma_start(out=sm[h][:], in_=by_token(sM)[:, 2 * h : 2 * h + 2, :])
+        def load_saved(half):
+            saved[half] = sbuf.tile([P, 2, D], F32, name="saved%d" % half)
+            nc.sync.dma_start(out=saved[half][:], in_=four_rows(sM)[:, 2 * half : 2 * half + 2, :])
 
-        def new_grouped(key, tag, bufs):
-            grouped[key] = stage.tile([P, CH * PACK], BF16, name="grouped", tag=tag, bufs=bufs, align_bytes=64)
-            return grouped[key]
+        def token_tile(name, c):
+            grouped[name, c] = sbuf.tile([P, CH * PACK], BF16, name="token", tag="token", bufs=TOKEN_BUFS, align_bytes=ALIGN)
+            return grouped[name, c]
 
         def interleave(name, c, engine):
-            rows_in = ds[c][:] if name == "ds" else raw[name][c]
-            dst = new_grouped((name, c), "tok", KB)
-            copy(engine, dst[:].rearrange("p (c i t) -> p c t i", i=4, t=PACK), rows_in.rearrange("p t (c i) -> p c t i", i=4))
-
-        def quant_tok(name, c):
-            quantise(q[name], c, grouped[name, c], E4M3 if name in ("xt", "xc") else E5M2)
+            out = token_tile(name, c)[:].rearrange("p (w i t) -> p w t i", i=4, t=PACK)
+            copy(engine, out, loaded[name, c][:].rearrange("p t (w i) -> p w t i", i=4))
 
         def make_ds(c):
+            loaded["ds", c] = sbuf.tile([P, PACK, CH], BF16, name="ds", tag="ds", bufs=DS_BUFS)
             for j in range(PACK):
-                nc.vector.scalar_tensor_tensor(out=ds[c][:, j, :], in0=raw["xt"][c][:, j, :], scalar=g1[:, j : j + 1],
-                                               in1=raw["g0"][c][:, j, :], op0=MULT, op1=ADD)
+                nc.vector.scalar_tensor_tensor(
+                    out=loaded["ds", c][:, j, :], in0=loaded["xt", c][:, j, :], scalar=g1[:, j : j + 1],
+                    in1=loaded["g0", c][:, j, :], op0=MULT, op1=ADD)
 
         def make_dc(c):
-            dst = new_grouped(("dc", c), "tok", KB)
-            nc.vector.tensor_tensor(out=dst[:].rearrange("p (w j) -> p w j", j=PACK),
-                                    in0=grouped["xc", c][:].rearrange("p (w j) -> p w j", j=PACK),
-                                    in1=g2[:].unsqueeze(1).broadcast_to([P, CH, PACK]), op=MULT)
+            nc.vector.tensor_tensor(
+                out=token_tile("dc", c)[:].rearrange("p (w t) -> p w t", t=PACK),
+                in0=grouped["xc", c][:].rearrange("p (w t) -> p w t", t=PACK),
+                in1=g2[:].unsqueeze(1).broadcast_to([P, CH, PACK]), op=MULT)
 
-        def turn(name, g, engines):
-            source = ds[g] if name == "dsT" else m_raw[int(name[2])]
-            base = 0 if name == "dsT" else g * CH // 2
+        def quantise(name, c):
+            nc.vector.quantize_mx(out=codes[name, c][:].bitcast(FORMAT[name]), scales=scales[name, c][:], in_=grouped[name, c][:])
+
+        reused = {}
+        for g in range(NCH):
+            reused["mT0", g] = ("xc0", "xt0", "g00")[g]
+            reused["mT1", g] = ("xc1", "xt1", "g01")[g]
+            reused["mT2", g] = ("m0_0", "m0_1", "m1_0")[g]
+
+        def transposes(name, g, half):
             if name == "dsT":
-                dst = new_grouped((name, g), "feat", FB)
+                rows, first = loaded["ds", g][:, 2 * half : 2 * half + 2, :], 0
             else:
-                if name not in wide:
-                    wide[name] = keep.tile([P, NCH * CH * PACK], BF16, name=name + "_grouped", tag=WSLOT[name], align_bytes=64)
-                dst = wide[name][:, g * CH * PACK : (g + 1) * CH * PACK]
-                grouped[name, g] = dst
-            words = dst[:].bitcast(F32)
-            banks = []
-            for b in range(2):
-                bank = psum.tile([P, 2, 2, P], F32, name="tbank", tag="tbank", bufs=TB)
-                banks.append(bank)
-                for r in range(2):
-                    row = source[:, 2 * b + r, :].bitcast(F32)
-                    for u in range(2):
-                        nc.tensor.transpose(bank[:, r, u, :], row[:, base + u : base + CH // 2 : 2], ident[:])
-            for b in range(2):
-                copy(engines[b], words[:, b * CH : (b + 1) * CH].rearrange("k (r p u) -> k r p u", r=2, u=2),
-                     banks[b][:].rearrange("k r u p -> k r p u"))
+                rows, first = loaded["m", int(name[2]), half][:], g * CH // 2
+            bank = psum.tile([P, 2, 2, P], F32, name="bank", tag="bank")
+            for r in range(2):
+                words = rows[:, r, :].bitcast(F32)
+                for u in range(2):
+                    nc.tensor.transpose(bank[:, r, u, :], words[:, first + u : first + CH // 2 : 2], ident[:])
 
-        def quant_feat(name, g):
-            quantise(q[name], g, grouped[name, g], E5M2 if name == "dsT" else E4M3)
+            def empty(engine):
+                if half == 0:
+                    tag = reused.get((name, g), "dsT%d" % g)
+                    grouped[name, g] = sbuf.tile([P, CH * PACK], BF16, name="feature", tag=tag, align_bytes=ALIGN)
+                out = grouped[name, g][:].bitcast(F32)[:, cols(half)].rearrange("k (r p u) -> k r p u", r=2, u=2)
+                copy(engine, out, bank[:].rearrange("k r u p -> k r p u"))
 
-        def mx(acc, left, lc, lw, lfmt, right, rc, rfmt, start, stop):
-            nc.tensor.matmul_mx(out=acc[:], lhsT=left[0][lc][:, lw].bitcast(lfmt), lhsT_scale=left[1][lc][:, lw],
-                                rhs=right[0][rc][:].bitcast(rfmt), rhs_scale=right[1][rc][:], start=start, stop=stop)
+            return empty
 
-        def dm_place(m, n):
-            if n == 0:
-                key = ("first", m // TILES)
-                if key not in rows:
-                    rows[key] = keep.tile([P, TILES, CH], F32, name="first%d" % key[1], tag="slot_f%d" % key[1], align_bytes=64)
-                return rows[key][:, m % TILES, :]
-            key = ("rest", m // 2)
-            if key not in rows:
-                rows[key] = keep.tile([P, 2, 2 * CH], F32, name="rest%d" % key[1], tag=RSLOT[key[1]], align_bytes=64)
-            return rows[key][:, m % 2, cols(n - 1)]
+        def mx_pass(bank, left, window, right, start, stop):
+            nc.tensor.matmul_mx(
+                out=bank[:], lhsT=codes[left][:, window].bitcast(FORMAT[left[0]]), lhsT_scale=scales[left][:, window],
+                rhs=codes[right][:].bitcast(FORMAT[right[0]]), rhs_scale=scales[right][:], start=start, stop=stop)
 
-        def dm_open(m, n):
-            w = slice((m % TILES) * P, (m % TILES + 1) * P)
-            opened[m, n] = psum.tile([P, CH], F32, name="acc", tag="acc", bufs=8 - TB)
-            mx(opened[m, n], q["xt"], m // TILES, w, E4M3, q["ds"], n, E5M2, True, False)
+        def dm_pair(a, b, half):
+            if half == 0:
+                blocks[a, b] = sbuf.tile([P, TILES, CH], F32, name="block", tag="block", bufs=BLOCK_BUFS)
+            tiles = (2 * half, 2 * half + 1)
+            banks = [psum.tile([P, CH], F32, name="bank", tag="bank") for m in tiles]
+            for m, bank in zip(tiles, banks):
+                mx_pass(bank, ("xt", a), slice(m * P, (m + 1) * P), ("ds", b), True, False)
+            for m, bank in zip(tiles, banks):
+                mx_pass(bank, ("xc", a), slice(m * P, (m + 1) * P), ("dc", b), False, True)
+            return [lambda engine, m=m, bank=bank: copy(engine, blocks[a, b][:, m, :], bank[:]) for m, bank in zip(tiles, banks)]
 
-        def dm_tile(m, n, engine):
-            w = slice((m % TILES) * P, (m % TILES + 1) * P)
-            if (m, n) not in opened:
-                dm_open(m, n)
-            acc = opened[m, n]
-            mx(acc, q["xc"], m // TILES, w, E4M3, q["dc"], n, E5M2, False, True)
-            copy(engine, dm_place(m, n), acc[:])
-
-        def store_first(c):
-            nc.sync.dma_start(out=out_1[cols(c), cols(0)].rearrange("(m p) w -> p m w", p=P), in_=rows["first", c][:])
-
-        def store_rest(h):
-            nc.sync.dma_start(out=out_1[2 * h * P : 2 * (h + 1) * P, CH:].rearrange("(m p) w -> p m w", p=P), in_=rows["rest", h][:])
-
-        def store_rest_row(m, c0, c1):
-            nc.sync.dma_start(out=out_1[m * P : (m + 1) * P, c0 * CH : c1 * CH], in_=rows["rest", m // 2][:, m % 2, (c0 - 1) * CH : (c1 - 1) * CH])
+        def store_block(a, b):
+            nc.sync.dma_start(out=out_1[cols(a), cols(b)].rearrange("(m p) w -> p m w", p=P), in_=blocks[a, b][:])
 
         def dx_tile(j, n):
-            acc = psum.tile([P, CH], F32, name="acc", tag="acc", bufs=8 - TB)
+            bank = psum.tile([P, CH], F32, name="bank", tag="bank")
             for g in range(NCH):
-                mx(acc, q["dsT"], g, slice(j * P, (j + 1) * P), E5M2, q["mT%d" % n], g, E4M3, g == 0, g == NCH - 1)
-            part = sm[j // 2][:, j % 2, cols(n)].rearrange("p (a r) -> p a r", r=PACK)
-            nc.vector.scalar_tensor_tensor(out=part, in0=part, scalar=g1[:, j : j + 1],
-                                           in1=acc[:].rearrange("p (r a) -> p a r", r=PACK), op0=MULT, op1=ADD)
+                mx_pass(bank, ("dsT", g), slice(j * P, (j + 1) * P), ("mT%d" % n, g), g == 0, g == NCH - 1)
+            part = saved[j // 2][:, j % 2, cols(n)].rearrange("p (i r) -> p i r", r=PACK)
+            nc.vector.scalar_tensor_tensor(
+                out=part, in0=part, scalar=g1[:, j : j + 1], in1=bank[:].rearrange("p (r i) -> p i r", r=PACK),
+                op0=MULT, op1=ADD)
 
-        def store_dx(j, c0, c1):
-            w = slice(c0 * CH, c1 * CH)
-            nc.sync.dma_start(out=by_token(out_0)[:, j, w], in_=sm[j // 2][:, j % 2, w])
+        def store_dx(j, window):
+            nc.sync.dma_start(out=four_rows(out_0)[:, j, window], in_=saved[j // 2][:, j % 2, window])
 
+        for c in range(NCH):
+            names = ("xt", "g0", "xc") if c == 0 else ("xt", "xc", "g0")
+            for name in names:
+                load_tokens(name, {"xt": x_train, "xc": x_test, "g0": grad_0}[name], c)
+            load_m(c, 0)
+            load_m(c, 1)
+        load_saved(0)
 
-        load("xt", 0, 1)
-        load("g0", 0, 1)
-        load("xc", 0, 1)
-        load_m(0)
-        load("xc", 1, 2)
-        load("xt", 1, 2)
-        load("xc", 2, 3)
-        load("xt", 2, 3)
-        load_m(1)
-        load("g0", 1, 3)
-        load_m(2)
-        interleave("xt", 0, "V")
-        interleave("xc", 0, "S")
+        interleave("xt", 0, "vector")
+        interleave("xc", 0, "scalar")
         make_ds(0)
-        quant_tok("xt", 0)
-        interleave("ds", 0, "V")
-        turn("dsT", 0, "SS")
-        quant_tok("xc", 0)
-        quant_tok("ds", 0)
+        quantise("xt", 0)
+        interleave("ds", 0, "vector")
         make_dc(0)
-        interleave("xc", 1, "V")
-        quant_tok("dc", 0)
-        turn("mT0", 0, "SS")
-        for m in range(4):
-            dm_open(m, 0)
-        turn("mT0", 1, "SS")
-        interleave("xt", 1, "V")
-        quant_tok("xc", 1)
-        quant_tok("xt", 1)
-        for m in range(4):
-            dm_tile(m, 0, "S")
-        turn("mT0", 2, "SS")
-        store_first(0)
-        interleave("xc", 2, "V")
-        interleave("xt", 2, "V")
-        quant_tok("xc", 2)
-        quant_tok("xt", 2)
-        for m in range(4, 8):
-            dm_tile(m, 0, "S")
-        store_first(1)
-        make_dc(1)
-        quant_feat("dsT", 0)
-        quant_tok("dc", 1)
-        make_ds(1)
-        dm_tile(8, 0, "S")
-        dm_tile(9, 0, "S")
-        turn("mT1", 0, "SS")
-        dm_tile(10, 0, "S")
-        turn("mT1", 1, "SS")
-        dm_tile(11, 0, "S")
-        turn("mT1", 2, "SS")
-        store_first(2)
-        load_sm(0)
-        load_sm(1)
-        quant_feat("mT0", 0)
-        interleave("ds", 1, "V")
-        quant_feat("mT0", 1)
-        quant_tok("ds", 1)
-        make_ds(2)
-        make_dc(2)
-        turn("mT2", 0, "SS")
-        dm_tile(0, 1, "S")
-        dm_tile(1, 1, "S")
-        turn("mT2", 1, "SS")
-        dm_tile(2, 1, "S")
-        dm_tile(3, 1, "S")
-        turn("mT2", 2, "SS")
-        turn("dsT", 1, "SS")
-        interleave("ds", 2, "V")
-        quant_tok("dc", 2)
-        quant_tok("ds", 2)
-        quant_feat("mT0", 2)
-        for g in range(3):
-            quant_feat("mT1", g)
-        for m in range(4):
-            dm_tile(m, 2, "S")
-            if m % 2:
-                store_rest(m // 2)
-        quant_feat("mT2", 0)
-        quant_feat("mT2", 1)
-        quant_feat("dsT", 1)
-        for m in range(4, 8):
-            dm_tile(m, 1, "S")
-            dm_tile(m, 2, "V" if m % 2 else "S")
-            if m % 2:
-                store_rest(m // 2)
-            if m == 5:
-                turn("dsT", 2, "SS")
-                quant_feat("mT2", 2)
-                quant_feat("dsT", 2)
-        for j in range(4):
-            for n in range(3):
+        quantise("ds", 0)
+        quantise("xc", 0)
+        quantise("dc", 0)
+
+        def m_banks(n, half):
+            return [("mT%d" % n, g, half) for g in range(NCH)]
+
+        def ds_banks(g):
+            return [("dsT", g, 0), ("dsT", g, 1)]
+
+        head = ds_banks(0) + m_banks(0, 0) + m_banks(0, 1)
+        for i, step in enumerate(head):
+            if i == len(head) // 2:
+                interleave("xt", 1, "scalar")
+            transposes(*step)("scalar")
+
+        for c in range(1, NCH):
+            if c > 1:
+                interleave("xt", c, "vector")
+            interleave("xc", c, "vector")
+            quantise("xt", c)
+            quantise("xc", c)
+            make_ds(c)
+            make_dc(c)
+            interleave("ds", c, "vector")
+            quantise("dc", c)
+            quantise("ds", c)
+
+        order = [(a, b) for c in range(NCH) for a, b in [(c, k) for k in range(c)] + [(k, c) for k in range(c + 1)]]
+        to_turn = m_banks(1, 0) + ds_banks(1) + m_banks(1, 1) + m_banks(2, 0) + m_banks(2, 1) + ds_banks(2)
+        to_quantise = [("dsT", 0)]
+        for n in range(NCH):
+            to_quantise.extend([("mT%d" % n, g) for g in range(NCH)] + ([("dsT", n)] if n else []))
+        shared = []
+
+        def empty_bank(empty, vector_free):
+            if not vector_free:
+                empty("scalar")
+                return
+            empty("scalar" if len(shared) % VECTOR_SHARE else "vector")
+            if len(shared) < len(to_quantise):
+                quantise(*to_quantise[len(shared)])
+            shared.append(empty)
+
+        for i, (a, b) in enumerate(order):
+            for half in range(2):
+                for empty in dm_pair(a, b, half):
+                    empty_bank(empty, max(a, b) == NCH - 1)
+                pair = 2 * i + half
+                for step in to_turn[WEAVE * (pair - 1) : WEAVE * pair] if pair else []:
+                    empty_bank(transposes(*step), max(a, b) == NCH - 1 or ((a, b, half) == (NCH - 2, NCH - 2, 1)))
+            store_block(a, b)
+            if i == 2:
+                load_saved(1)
+
+        for j in range(PACK):
+            for n in range(NCH):
                 dx_tile(j, n)
-            store_dx(j, 0, 3)
-            dm_tile(8 + j, 1, "S")
-            if j == 3:
-                store_rest_row(8 + j, 1, 2)
-            dm_tile(8 + j, 2, "S")
-            if j == 3:
-                store_rest_row(8 + j, 2, 3)
-            else:
-                store_rest_row(8 + j, 1, 3)
+                if j == PACK - 1:
+                    store_dx(j, cols(n))
+            if j < PACK - 1:
+                store_dx(j, slice(0, D))

@@ -23,12 +23,14 @@ TILES = CH // P
 ALIGN = 64
 FORMAT = {"xt": E4M3, "xc": E4M3, "mT0": E4M3, "mT1": E4M3, "mT2": E4M3, "ds": E5M2, "dc": E5M2, "dsT": E5M2}
 
+LAST = NCH - 1
+
 BANKS = 8
 TOKEN_BUFS = 5
 DS_BUFS = 2
-BLOCK_BUFS = 5
+HEAD = 6
+HEAD_SPLIT = 4
 WEAVE = 2
-VECTOR_SHARE = 3
 
 
 def tile_rbfnet_pa_v_kernel(tc, x_train, x_test, M, sM, grad_0, grad_1, grad_2, out_0, out_1):
@@ -38,8 +40,8 @@ def tile_rbfnet_pa_v_kernel(tc, x_train, x_test, M, sM, grad_0, grad_1, grad_2, 
         psum = ctx.enter_context(tc.psum_pool(name="psum", bufs=BANKS))
         ctx.enter_context(tc.manual_schedule())
 
-        def cols(c):
-            return slice(c * CH, (c + 1) * CH)
+        def span(i, width=CH):
+            return slice(i * width, (i + 1) * width)
 
         def four_rows(t):
             return t.rearrange("(p j) w -> p j w", j=PACK)
@@ -62,19 +64,27 @@ def tile_rbfnet_pa_v_kernel(tc, x_train, x_test, M, sM, grad_0, grad_1, grad_2, 
             for c in range(NCH):
                 codes[name, c] = sbuf.tile([P, CH], U32, name="%s_codes%d" % (name, c), align_bytes=ALIGN)
                 scales[name, c] = sbuf.tile([P, CH], U8, name="%s_scales%d" % (name, c), align_bytes=ALIGN)
-        loaded, grouped, blocks, saved = {}, {}, {}, {}
+        plain, grouped, sorted_m, staged = {}, {}, {}, {}
 
-        def load_tokens(name, source, c):
-            loaded[name, c] = sbuf.tile([P, PACK, CH], BF16, name=name, tag="%s%d" % (name, c), align_bytes=ALIGN)
-            nc.sync.dma_start(out=loaded[name, c][:], in_=four_rows(source)[:, :, cols(c)])
+        feature_tags = {
+            "dsT": ("dsT0", "dsT1", "dsT2"),
+            "mT0": ("xc0", "xt0", "g00"),
+            "mT1": ("xc1", "xt1", "g01"),
+            "mT2": ("m1_0", "m1_1", "m2_0"),
+        }
+        sorted_tags = ("m0_0", "m0_1")
+        row_tags = ("m0_0", "m0_1", "m2_1", "row")
 
-        def load_m(n, half):
-            loaded["m", n, half] = sbuf.tile([P, 2, D], BF16, name="m", tag="m%d_%d" % (n, half), align_bytes=ALIGN)
-            nc.sync.dma_start(out=loaded["m", n, half][:], in_=four_rows(M[cols(n), :])[:, 2 * half : 2 * half + 2, :])
+        def load_tokens(names, c):
+            for name in names:
+                source = {"xt": x_train, "xc": x_test, "g0": grad_0}[name]
+                plain[name, c] = sbuf.tile([P, PACK, CH], BF16, name=name, tag="%s%d" % (name, c), align_bytes=ALIGN)
+                nc.sync.dma_start(out=plain[name, c][:], in_=four_rows(source)[:, :, span(c)])
 
-        def load_saved(half):
-            saved[half] = sbuf.tile([P, 2, D], F32, name="saved%d" % half)
-            nc.sync.dma_start(out=saved[half][:], in_=four_rows(sM)[:, 2 * half : 2 * half + 2, :])
+        def load_m(n):
+            for half in range(2):
+                plain["m", n, half] = sbuf.tile([P, 2, D], BF16, name="m", tag="m%d_%d" % (n, half), align_bytes=ALIGN)
+                nc.sync.dma_start(out=plain["m", n, half][:], in_=four_rows(M[span(n), :])[:, span(half, 2), :])
 
         def token_tile(name, c):
             grouped[name, c] = sbuf.tile([P, CH * PACK], BF16, name="token", tag="token", bufs=TOKEN_BUFS, align_bytes=ALIGN)
@@ -82,14 +92,14 @@ def tile_rbfnet_pa_v_kernel(tc, x_train, x_test, M, sM, grad_0, grad_1, grad_2, 
 
         def interleave(name, c, engine):
             out = token_tile(name, c)[:].rearrange("p (w i t) -> p w t i", i=4, t=PACK)
-            copy(engine, out, loaded[name, c][:].rearrange("p t (w i) -> p w t i", i=4))
+            copy(engine, out, plain[name, c][:].rearrange("p t (w i) -> p w t i", i=4))
 
         def make_ds(c):
-            loaded["ds", c] = sbuf.tile([P, PACK, CH], BF16, name="ds", tag="ds", bufs=DS_BUFS)
+            plain["ds", c] = sbuf.tile([P, PACK, CH], BF16, name="ds", tag="ds", bufs=DS_BUFS)
             for j in range(PACK):
                 nc.vector.scalar_tensor_tensor(
-                    out=loaded["ds", c][:, j, :], in0=loaded["xt", c][:, j, :], scalar=g1[:, j : j + 1],
-                    in1=loaded["g0", c][:, j, :], op0=MULT, op1=ADD)
+                    out=plain["ds", c][:, j, :], in0=plain["xt", c][:, j, :], scalar=g1[:, j : j + 1],
+                    in1=plain["g0", c][:, j, :], op0=MULT, op1=ADD)
 
         def make_dc(c):
             nc.vector.tensor_tensor(
@@ -100,28 +110,40 @@ def tile_rbfnet_pa_v_kernel(tc, x_train, x_test, M, sM, grad_0, grad_1, grad_2, 
         def quantise(name, c):
             nc.vector.quantize_mx(out=codes[name, c][:].bitcast(FORMAT[name]), scales=scales[name, c][:], in_=grouped[name, c][:])
 
-        reused = {}
-        for g in range(NCH):
-            reused["mT0", g] = ("xc0", "xt0", "g00")[g]
-            reused["mT1", g] = ("xc1", "xt1", "g01")[g]
-            reused["mT2", g] = ("m0_0", "m0_1", "m1_0")[g]
+        def finish_chunk(c):
+            quantise("xt", c)
+            quantise("xc", c)
+            make_ds(c)
+            make_dc(c)
+            interleave("ds", c, "vector")
+            quantise("dc", c)
+            quantise("ds", c)
+
+        def sort_words(half):
+            sorted_m[half] = sbuf.tile([P, D], F32, name="sorted", tag=sorted_tags[half], align_bytes=ALIGN)
+            words = plain["m", LAST, half][:].rearrange("p r w -> p (r w)").bitcast(F32)
+            nc.vector.tensor_copy(
+                out=sorted_m[half][:].rearrange("p (q u w) -> p q u w", u=2, w=P),
+                in_=words.rearrange("p (q w u) -> p q u w", u=2, w=P))
+
+        def word_block(name, g, half, r, u):
+            if name == "dsT":
+                return plain["ds", g][:, 2 * half + r, :].bitcast(F32)[:, u : 2 * P : 2]
+            n = int(name[2])
+            if n == LAST:
+                return sorted_m[half][:, span((r * NCH + g) * 2 + u, P)]
+            return plain["m", n, half][:, r, :].bitcast(F32)[:, 2 * P * g + u : 2 * P * (g + 1) : 2]
 
         def transposes(name, g, half):
-            if name == "dsT":
-                rows, first = loaded["ds", g][:, 2 * half : 2 * half + 2, :], 0
-            else:
-                rows, first = loaded["m", int(name[2]), half][:], g * CH // 2
             bank = psum.tile([P, 2, 2, P], F32, name="bank", tag="bank")
             for r in range(2):
-                words = rows[:, r, :].bitcast(F32)
                 for u in range(2):
-                    nc.tensor.transpose(bank[:, r, u, :], words[:, first + u : first + CH // 2 : 2], ident[:])
+                    nc.tensor.transpose(bank[:, r, u, :], word_block(name, g, half, r, u), ident[:])
 
             def empty(engine):
                 if half == 0:
-                    tag = reused.get((name, g), "dsT%d" % g)
-                    grouped[name, g] = sbuf.tile([P, CH * PACK], BF16, name="feature", tag=tag, align_bytes=ALIGN)
-                out = grouped[name, g][:].bitcast(F32)[:, cols(half)].rearrange("k (r p u) -> k r p u", r=2, u=2)
+                    grouped[name, g] = sbuf.tile([P, CH * PACK], BF16, name="feature", tag=feature_tags[name][g], align_bytes=ALIGN)
+                out = grouped[name, g][:].bitcast(F32)[:, span(half)].rearrange("k (r p u) -> k r p u", r=2, u=2)
                 copy(engine, out, bank[:].rearrange("k r u p -> k r p u"))
 
             return empty
@@ -131,39 +153,56 @@ def tile_rbfnet_pa_v_kernel(tc, x_train, x_test, M, sM, grad_0, grad_1, grad_2, 
                 out=bank[:], lhsT=codes[left][:, window].bitcast(FORMAT[left[0]]), lhsT_scale=scales[left][:, window],
                 rhs=codes[right][:].bitcast(FORMAT[right[0]]), rhs_scale=scales[right][:], start=start, stop=stop)
 
+        def stage(a, b, m):
+            if a == LAST:
+                if b == 0:
+                    staged[a, m] = sbuf.tile([P, D], F32, name="row", tag=row_tags[m], align_bytes=ALIGN)
+                return staged[a, m][:, span(b)]
+            first = LAST if b == LAST else 0
+            if b == first and m % 2 == 0:
+                width = CH if b == LAST else LAST * CH
+                staged[a, m // 2] = sbuf.tile([P, 2, width], F32, name="part", tag="part%d_%d" % (a, m // 2))
+            return staged[a, m // 2][:, m % 2, span(b - first)]
+
+        def store_dm(a, b, half):
+            rows = out_1[a * CH + 2 * half * P : a * CH + 2 * (half + 1) * P, :].rearrange("(m p) w -> p m w", p=P)
+            if a == LAST and b == LAST:
+                for m in range(2):
+                    nc.sync.dma_start(out=rows[:, m, :], in_=staged[a, 2 * half + m][:])
+            elif a < LAST and b == LAST - 1:
+                nc.sync.dma_start(out=rows[:, :, : LAST * CH], in_=staged[a, half][:])
+            elif a < LAST and b == LAST:
+                nc.sync.dma_start(out=rows[:, :, span(LAST)], in_=staged[a, half][:])
+
         def dm_pair(a, b, half):
-            if half == 0:
-                blocks[a, b] = sbuf.tile([P, TILES, CH], F32, name="block", tag="block", bufs=BLOCK_BUFS)
             tiles = (2 * half, 2 * half + 1)
             banks = [psum.tile([P, CH], F32, name="bank", tag="bank") for m in tiles]
             for m, bank in zip(tiles, banks):
-                mx_pass(bank, ("xt", a), slice(m * P, (m + 1) * P), ("ds", b), True, False)
+                mx_pass(bank, ("xt", a), span(m, P), ("ds", b), True, False)
             for m, bank in zip(tiles, banks):
-                mx_pass(bank, ("xc", a), slice(m * P, (m + 1) * P), ("dc", b), False, True)
-            return [lambda engine, m=m, bank=bank: copy(engine, blocks[a, b][:, m, :], bank[:]) for m, bank in zip(tiles, banks)]
-
-        def store_block(a, b):
-            nc.sync.dma_start(out=out_1[cols(a), cols(b)].rearrange("(m p) w -> p m w", p=P), in_=blocks[a, b][:])
+                mx_pass(bank, ("xc", a), span(m, P), ("dc", b), False, True)
+            return [lambda engine, m=m, bank=bank: copy(engine, stage(a, b, m), bank[:]) for m, bank in zip(tiles, banks)]
 
         def dx_tile(j, n):
             bank = psum.tile([P, CH], F32, name="bank", tag="bank")
             for g in range(NCH):
-                mx_pass(bank, ("dsT", g), slice(j * P, (j + 1) * P), ("mT%d" % n, g), g == 0, g == NCH - 1)
-            part = saved[j // 2][:, j % 2, cols(n)].rearrange("p (i r) -> p i r", r=PACK)
+                mx_pass(bank, ("dsT", g), span(j, P), ("mT%d" % n, g), g == 0, g == LAST)
+            part = saved[:, j, span(n)].rearrange("p (i r) -> p i r", r=PACK)
             nc.vector.scalar_tensor_tensor(
                 out=part, in0=part, scalar=g1[:, j : j + 1], in1=bank[:].rearrange("p (r i) -> p i r", r=PACK),
                 op0=MULT, op1=ADD)
 
         def store_dx(j, window):
-            nc.sync.dma_start(out=four_rows(out_0)[:, j, window], in_=saved[j // 2][:, j % 2, window])
+            nc.sync.dma_start(out=four_rows(out_0)[:, j, window], in_=saved[:, j, window])
 
-        for c in range(NCH):
-            names = ("xt", "g0", "xc") if c == 0 else ("xt", "xc", "g0")
-            for name in names:
-                load_tokens(name, {"xt": x_train, "xc": x_test, "g0": grad_0}[name], c)
-            load_m(c, 0)
-            load_m(c, 1)
-        load_saved(0)
+        load_tokens(("xt", "g0", "xc"), 0)
+        load_m(0)
+        load_tokens(("xt", "xc", "g0"), 1)
+        load_m(1)
+        load_m(2)
+        load_tokens(("xt", "xc", "g0"), 2)
+        saved = sbuf.tile([P, PACK, D], F32, name="saved")
+        nc.sync.dma_start(out=saved[:], in_=four_rows(sM))
 
         interleave("xt", 0, "vector")
         interleave("xc", 0, "scalar")
@@ -181,55 +220,52 @@ def tile_rbfnet_pa_v_kernel(tc, x_train, x_test, M, sM, grad_0, grad_1, grad_2, 
         def ds_banks(g):
             return [("dsT", g, 0), ("dsT", g, 1)]
 
-        head = ds_banks(0) + m_banks(0, 0) + m_banks(0, 1)
-        for i, step in enumerate(head):
-            if i == len(head) // 2:
+        to_turn = ds_banks(0) + m_banks(0, 0) + m_banks(0, 1) + m_banks(1, 0) + ds_banks(1) + m_banks(1, 1)
+        to_turn.extend(m_banks(2, 0) + m_banks(2, 1) + ds_banks(2))
+        for i, step in enumerate(to_turn[:HEAD]):
+            if i == HEAD_SPLIT:
                 interleave("xt", 1, "scalar")
             transposes(*step)("scalar")
+        interleave("xc", 1, "vector")
+        finish_chunk(1)
 
-        for c in range(1, NCH):
-            if c > 1:
-                interleave("xt", c, "vector")
-            interleave("xc", c, "vector")
-            quantise("xt", c)
-            quantise("xc", c)
-            make_ds(c)
-            make_dc(c)
-            interleave("ds", c, "vector")
-            quantise("dc", c)
-            quantise("ds", c)
-
-        order = [(a, b) for c in range(NCH) for a, b in [(c, k) for k in range(c)] + [(k, c) for k in range(c + 1)]]
-        to_turn = m_banks(1, 0) + ds_banks(1) + m_banks(1, 1) + m_banks(2, 0) + m_banks(2, 1) + ds_banks(2)
+        early = [(a, b, half) for b in range(LAST) for a in range(LAST) for half in range(2)]
+        late = [(LAST, b, half) for half in range(2) for b in range(NCH)]
+        late.extend([(a, LAST, half) for a in range(LAST) for half in range(2)])
         to_quantise = [("dsT", 0)]
         for n in range(NCH):
             to_quantise.extend([("mT%d" % n, g) for g in range(NCH)] + ([("dsT", n)] if n else []))
-        shared = []
+        emptied_late = []
 
-        def empty_bank(empty, vector_free):
-            if not vector_free:
+        def empty_late(empty):
+            i = len(emptied_late)
+            emptied_late.append(empty)
+            if i < len(to_quantise):
                 empty("scalar")
-                return
-            empty("scalar" if len(shared) % VECTOR_SHARE else "vector")
-            if len(shared) < len(to_quantise):
-                quantise(*to_quantise[len(shared)])
-            shared.append(empty)
+                quantise(*to_quantise[i])
+            else:
+                empty("scalar" if i % 2 else "vector")
 
-        for i, (a, b) in enumerate(order):
-            for half in range(2):
-                for empty in dm_pair(a, b, half):
-                    empty_bank(empty, max(a, b) == NCH - 1)
-                pair = 2 * i + half
-                for step in to_turn[WEAVE * (pair - 1) : WEAVE * pair] if pair else []:
-                    empty_bank(transposes(*step), max(a, b) == NCH - 1 or ((a, b, half) == (NCH - 2, NCH - 2, 1)))
-            store_block(a, b)
-            if i == 2:
-                load_saved(1)
+        def empty_early(empty):
+            empty("scalar")
+
+        for i, (a, b, half) in enumerate(early + late):
+            for empty in dm_pair(a, b, half):
+                (empty_late if i >= len(early) else empty_early)(empty)
+            for step in to_turn[HEAD + WEAVE * i : HEAD + WEAVE * (i + 1)]:
+                (empty_late if i + 1 >= len(early) else empty_early)(transposes(*step))
+            store_dm(a, b, half)
+            if (a, b, half) == (0, 0, 1):
+                sort_words(0)
+                sort_words(1)
+                interleave("xt", LAST, "vector")
+                interleave("xc", LAST, "vector")
+                finish_chunk(LAST)
 
         for j in range(PACK):
             for n in range(NCH):
                 dx_tile(j, n)
                 if j == PACK - 1:
-                    store_dx(j, cols(n))
+                    store_dx(j, span(n))
             if j < PACK - 1:
                 store_dx(j, slice(0, D))

from contextlib import ExitStack

import concourse.mybir as mybir
from concourse.masks import make_identity

NTR, NTE, D = 512, 512, 1536
FLOPS = 2 * NTR * D * D + 2 * (NTR + NTE) * D * D

F32 = mybir.dt.float32
BF16 = mybir.dt.bfloat16
U32 = mybir.dt.uint32
U8 = mybir.dt.uint8
E4M3 = mybir.dt.float8_e4m3fn_x4
E5M2 = mybir.dt.float8_e5m2_x4
MULT = mybir.AluOpType.mult
ADD = mybir.AluOpType.add

P = 128
PACK = 4
CH = P * PACK
NCH = D // CH
TILES = CH // P
ALIGN = 64
FORMAT = {"xt": E4M3, "xc": E4M3, "mT0": E4M3, "mT1": E4M3, "mT2": E4M3, "ds": E5M2, "dc": E5M2, "dsT": E5M2}

LAST = NCH - 1

BANKS = 8
TOKEN_BUFS = 5
DS_BUFS = 2
HEAD = 6
HEAD_SPLIT = 4
WEAVE = 2


def tile_rbfnet_pa_v_kernel(tc, x_train, x_test, M, sM, grad_0, grad_1, grad_2, out_0, out_1):
    nc = tc.nc
    with ExitStack() as ctx:
        sbuf = ctx.enter_context(tc.tile_pool(name="sbuf", bufs=1))
        psum = ctx.enter_context(tc.psum_pool(name="psum", bufs=BANKS))
        ctx.enter_context(tc.manual_schedule())

        def span(i, width=CH):
            return slice(i * width, (i + 1) * width)

        def four_rows(t):
            return t.rearrange("(p j) w -> p j w", j=PACK)

        def copy(engine, out, in_):
            if engine == "vector":
                nc.vector.tensor_copy(out=out, in_=in_)
            else:
                nc.scalar.copy(out=out, in_=in_)

        ident = sbuf.tile([P, P], F32, name="ident")
        make_identity(nc, ident[:])
        g1 = sbuf.tile([P, PACK], BF16, name="g1")
        g2 = sbuf.tile([P, PACK], BF16, name="g2")
        nc.scalar.dma_start(out=g1[:], in_=grad_1.rearrange("(p j) -> p j", j=PACK))
        nc.scalar.dma_start(out=g2[:], in_=grad_2.rearrange("(p j) -> p j", j=PACK))

        codes, scales = {}, {}
        for name in FORMAT:
            for c in range(NCH):
                codes[name, c] = sbuf.tile([P, CH], U32, name="%s_codes%d" % (name, c), align_bytes=ALIGN)
                scales[name, c] = sbuf.tile([P, CH], U8, name="%s_scales%d" % (name, c), align_bytes=ALIGN)
        plain, grouped, sorted_m, staged = {}, {}, {}, {}

        feature_tags = {
            "dsT": ("dsT0", "dsT1", "dsT2"),
            "mT0": ("xc0", "xt0", "g00"),
            "mT1": ("xc1", "xt1", "g01"),
            "mT2": ("m1_0", "m1_1", "m2_0"),
        }
        sorted_tags = ("m0_0", "m0_1")
        row_tags = ("m0_0", "m0_1", "m2_1", "row")

        def load_tokens(names, c):
            for name in names:
                source = {"xt": x_train, "xc": x_test, "g0": grad_0}[name]
                plain[name, c] = sbuf.tile([P, PACK, CH], BF16, name=name, tag="%s%d" % (name, c), align_bytes=ALIGN)
                nc.sync.dma_start(out=plain[name, c][:], in_=four_rows(source)[:, :, span(c)])

        def load_m(n):
            for half in range(2):
                plain["m", n, half] = sbuf.tile([P, 2, D], BF16, name="m", tag="m%d_%d" % (n, half), align_bytes=ALIGN)
                nc.sync.dma_start(out=plain["m", n, half][:], in_=four_rows(M[span(n), :])[:, span(half, 2), :])

        def token_tile(name, c):
            grouped[name, c] = sbuf.tile([P, CH * PACK], BF16, name="token", tag="token", bufs=TOKEN_BUFS, align_bytes=ALIGN)
            return grouped[name, c]

        def interleave(name, c, engine):
            out = token_tile(name, c)[:].rearrange("p (w i t) -> p w t i", i=4, t=PACK)
            copy(engine, out, plain[name, c][:].rearrange("p t (w i) -> p w t i", i=4))

        def make_ds(c):
            plain["ds", c] = sbuf.tile([P, PACK, CH], BF16, name="ds", tag="ds", bufs=DS_BUFS)
            for j in range(PACK):
                nc.vector.scalar_tensor_tensor(
                    out=plain["ds", c][:, j, :], in0=plain["xt", c][:, j, :], scalar=g1[:, j : j + 1],
                    in1=plain["g0", c][:, j, :], op0=MULT, op1=ADD)

        def make_dc(c):
            nc.vector.tensor_tensor(
                out=token_tile("dc", c)[:].rearrange("p (w t) -> p w t", t=PACK),
                in0=grouped["xc", c][:].rearrange("p (w t) -> p w t", t=PACK),
                in1=g2[:].unsqueeze(1).broadcast_to([P, CH, PACK]), op=MULT)

        def quantise(name, c):
            nc.vector.quantize_mx(out=codes[name, c][:].bitcast(FORMAT[name]), scales=scales[name, c][:], in_=grouped[name, c][:])

        def finish_chunk(c):
            quantise("xt", c)
            quantise("xc", c)
            make_ds(c)
            make_dc(c)
            interleave("ds", c, "vector")
            quantise("dc", c)
            quantise("ds", c)

        def sort_words(half):
            sorted_m[half] = sbuf.tile([P, D], F32, name="sorted", tag=sorted_tags[half], align_bytes=ALIGN)
            words = plain["m", LAST, half][:].rearrange("p r w -> p (r w)").bitcast(F32)
            nc.vector.tensor_copy(
                out=sorted_m[half][:].rearrange("p (q u w) -> p q u w", u=2, w=P),
                in_=words.rearrange("p (q w u) -> p q u w", u=2, w=P))

        def word_block(name, g, half, r, u):
            if name == "dsT":
                return plain["ds", g][:, 2 * half + r, :].bitcast(F32)[:, u : 2 * P : 2]
            n = int(name[2])
            if n == LAST:
                return sorted_m[half][:, span((r * NCH + g) * 2 + u, P)]
            return plain["m", n, half][:, r, :].bitcast(F32)[:, 2 * P * g + u : 2 * P * (g + 1) : 2]

        def transposes(name, g, half):
            bank = psum.tile([P, 2, 2, P], F32, name="bank", tag="bank")
            for r in range(2):
                for u in range(2):
                    nc.tensor.transpose(bank[:, r, u, :], word_block(name, g, half, r, u), ident[:])

            def empty(engine):
                if half == 0:
                    grouped[name, g] = sbuf.tile([P, CH * PACK], BF16, name="feature", tag=feature_tags[name][g], align_bytes=ALIGN)
                out = grouped[name, g][:].bitcast(F32)[:, span(half)].rearrange("k (r p u) -> k r p u", r=2, u=2)
                copy(engine, out, bank[:].rearrange("k r u p -> k r p u"))

            return empty

        def mx_pass(bank, left, window, right, start, stop):
            nc.tensor.matmul_mx(
                out=bank[:], lhsT=codes[left][:, window].bitcast(FORMAT[left[0]]), lhsT_scale=scales[left][:, window],
                rhs=codes[right][:].bitcast(FORMAT[right[0]]), rhs_scale=scales[right][:], start=start, stop=stop)

        def stage(a, b, m):
            if a == LAST:
                if b == 0:
                    staged[a, m] = sbuf.tile([P, D], F32, name="row", tag=row_tags[m], align_bytes=ALIGN)
                return staged[a, m][:, span(b)]
            first = LAST if b == LAST else 0
            if b == first and m % 2 == 0:
                width = CH if b == LAST else LAST * CH
                staged[a, m // 2] = sbuf.tile([P, 2, width], F32, name="part", tag="part%d_%d" % (a, m // 2))
            return staged[a, m // 2][:, m % 2, span(b - first)]

        def store_dm(a, b, half):
            rows = out_1[a * CH + 2 * half * P : a * CH + 2 * (half + 1) * P, :].rearrange("(m p) w -> p m w", p=P)
            if a == LAST and b == LAST:
                for m in range(2):
                    nc.sync.dma_start(out=rows[:, m, :], in_=staged[a, 2 * half + m][:])
            elif a < LAST and b == LAST - 1:
                nc.sync.dma_start(out=rows[:, :, : LAST * CH], in_=staged[a, half][:])
            elif a < LAST and b == LAST:
                nc.sync.dma_start(out=rows[:, :, span(LAST)], in_=staged[a, half][:])

        def dm_pair(a, b, half):
            tiles = (2 * half, 2 * half + 1)
            banks = [psum.tile([P, CH], F32, name="bank", tag="bank") for m in tiles]
            for m, bank in zip(tiles, banks):
                mx_pass(bank, ("xt", a), span(m, P), ("ds", b), True, False)
            for m, bank in zip(tiles, banks):
                mx_pass(bank, ("xc", a), span(m, P), ("dc", b), False, True)
            return [lambda engine, m=m, bank=bank: copy(engine, stage(a, b, m), bank[:]) for m, bank in zip(tiles, banks)]

        def dx_tile(j, n):
            bank = psum.tile([P, CH], F32, name="bank", tag="bank")
            for g in range(NCH):
                mx_pass(bank, ("dsT", g), span(j, P), ("mT%d" % n, g), g == 0, g == LAST)
            part = saved[:, j, span(n)].rearrange("p (i r) -> p i r", r=PACK)
            nc.vector.scalar_tensor_tensor(
                out=part, in0=part, scalar=g1[:, j : j + 1], in1=bank[:].rearrange("p (r i) -> p i r", r=PACK),
                op0=MULT, op1=ADD)

        def store_dx(j, window):
            nc.sync.dma_start(out=four_rows(out_0)[:, j, window], in_=saved[:, j, window])

        load_tokens(("xt", "g0", "xc"), 0)
        load_m(0)
        load_tokens(("xt", "xc", "g0"), 1)
        load_m(1)
        load_m(2)
        load_tokens(("xt", "xc", "g0"), 2)
        saved = sbuf.tile([P, PACK, D], F32, name="saved")
        nc.sync.dma_start(out=saved[:], in_=four_rows(sM))

        interleave("xt", 0, "vector")
        interleave("xc", 0, "scalar")
        make_ds(0)
        quantise("xt", 0)
        interleave("ds", 0, "vector")
        make_dc(0)
        quantise("ds", 0)
        quantise("xc", 0)
        quantise("dc", 0)

        def m_banks(n, half):
            return [("mT%d" % n, g, half) for g in range(NCH)]

        def ds_banks(g):
            return [("dsT", g, 0), ("dsT", g, 1)]

        to_turn = ds_banks(0) + m_banks(0, 0) + m_banks(0, 1) + m_banks(1, 0) + ds_banks(1) + m_banks(1, 1)
        to_turn.extend(m_banks(2, 0) + m_banks(2, 1) + ds_banks(2))
        for i, step in enumerate(to_turn[:HEAD]):
            if i == HEAD_SPLIT:
                interleave("xt", 1, "scalar")
            transposes(*step)("scalar")
        interleave("xc", 1, "vector")
        finish_chunk(1)

        early = [(a, b, half) for b in range(LAST) for a in range(LAST) for half in range(2)]
        late = [(LAST, b, half) for half in range(2) for b in range(NCH)]
        late.extend([(a, LAST, half) for a in range(LAST) for half in range(2)])
        to_quantise = [("dsT", 0)]
        for n in range(NCH):
            to_quantise.extend([("mT%d" % n, g) for g in range(NCH)] + ([("dsT", n)] if n else []))
        emptied_late = []

        def empty_late(empty):
            i = len(emptied_late)
            emptied_late.append(empty)
            if i < len(to_quantise):
                empty("scalar")
                quantise(*to_quantise[i])
            else:
                empty("scalar" if i % 2 else "vector")

        def empty_early(empty):
            empty("scalar")

        for i, (a, b, half) in enumerate(early + late):
            for empty in dm_pair(a, b, half):
                (empty_late if i >= len(early) else empty_early)(empty)
            for step in to_turn[HEAD + WEAVE * i : HEAD + WEAVE * (i + 1)]:
                (empty_late if i + 1 >= len(early) else empty_early)(transposes(*step))
            store_dm(a, b, half)
            if (a, b, half) == (0, 0, 1):
                sort_words(0)
                sort_words(1)
                interleave("xt", LAST, "vector")
                interleave("xc", LAST, "vector")
                finish_chunk(LAST)

        for j in range(PACK):
            for n in range(NCH):
                dx_tile(j, n)
                if j == PACK - 1:
                    store_dx(j, span(n))
            if j < PACK - 1:
                store_dx(j, slice(0, D))
